import numpy as np
import ml_dtypes


def mxq(x, axis, fmt="e4m3"):
    dtype, down = {"e4m3": (ml_dtypes.float8_e4m3fn, 7), "e5m2": (ml_dtypes.float8_e5m2, 14)}[fmt]
    v = np.moveaxis(np.asarray(x, np.float32).astype(ml_dtypes.bfloat16).astype(np.float64), axis, -1)
    blocks = v.reshape(v.shape[:-1] + (-1, 32))
    amax = np.abs(blocks).max(-1, keepdims=True)
    byte = np.maximum(np.where(amax > 0, np.frexp(amax)[1] - 1 + 127, 0) - down, 1)
    scale = np.exp2(byte - 127.0)
    codes = (blocks / scale).astype(np.float32).astype(dtype).astype(np.float64)
    return np.moveaxis((codes * scale).reshape(v.shape), -1, axis)


WIDE = False


def mx_kscale(k):
    if not WIDE:
        return np.ones(k)
    levels = np.array([10, -10, 5, -5, 0])
    a = np.random.permutation(np.resize(levels, k // 512 * 4)).reshape(k // 512, 4)
    idx = np.arange(k)
    return np.exp2(a[idx // 512, idx % 128 // 32])


BF16 = ml_dtypes.bfloat16


def bf(x):
    return np.asarray(x, np.float32).astype(BF16)


def f64(x):
    return np.asarray(x).astype(np.float64)


N, C, P, D = 512, 128, 7, 1024
SCALE = 1.0 / np.sqrt(D)


def setup_inputs():
    s, t = mx_kscale(D), mx_kscale(D)
    return {"h": bf(np.random.standard_normal((N, D)) * s),
            "w_q": bf(np.random.standard_normal((D, D)) * 1.6 / np.sqrt(D) / s * t[:, None]),
            "b_q": bf(np.random.standard_normal(D) * 0.2 * t),
            "w_k": bf(np.random.standard_normal((D, D)) * 1.6 / np.sqrt(D) / s / t[:, None]),
            "b_k": bf(np.random.standard_normal(D) * 0.2 / t)}


def reference(h, w_q, b_q, w_k, b_k):
    hq = mxq(f64(h), 1, "e4m3")
    q = (hq @ mxq(f64(w_q).T, 0, "e4m3")) + f64(b_q)
    k = (hq @ mxq(f64(w_k).T, 0, "e4m3")) + f64(b_k)
    return (mxq(q, 1, "e4m3") @ mxq(k.T, 0, "e4m3")) * SCALE

@@ -1,0 +1,183 @@
+from contextlib import ExitStack
+import math
+
+import concourse.mybir as mybir
+from concourse.masks import make_identity
+
+F32 = mybir.dt.float32
+BF16 = mybir.dt.bfloat16
+U32 = mybir.dt.uint32
+U8 = mybir.dt.uint8
+FP8X4 = mybir.dt.float8_e4m3fn_x4
+
+P = 128
+PACK = 4
+K_PASS = P * PACK
+PROPOSALS = 512
+FEATURES = 1024
+PASSES = FEATURES // K_PASS
+GROUPS = PROPOSALS // P
+WORDS = FEATURES // 2
+LOAD_ROWS = 2
+SCALE = 1.0 / math.sqrt(FEATURES)
+assert GROUPS == PACK
+
+FLOPS = 2 * 2 * PROPOSALS * FEATURES * FEATURES + 2 * PROPOSALS * PROPOSALS * FEATURES
+
+
+def transpose_rows(nc, turned_pool, keep, rows, identity, label):
+    words = rows.bitcast(F32)
+    turned = turned_pool.tile([P, WORDS], F32, tag="bank")
+    for c in range(WORDS // P):
+        cols = slice(c * P, (c + 1) * P)
+        nc.tensor.transpose(turned[:, cols], words[:, cols], identity[:])
+    grouped = keep.tile([P, FEATURES], BF16, name="grouped_" + label, align_bytes=64)
+    nc.scalar.copy(
+        out=grouped[:].bitcast(F32).rearrange("p (g r u) -> p g r u", g=PASSES, u=2),
+        in_=turned[:].rearrange("p (g u r) -> p g r u", g=PASSES, u=2),
+    )
+    return grouped
+
+
+def quantise_rows(nc, keep, grouped, label):
+    codes = keep.tile([P, PASSES * P], U32, name="codes_" + label, align_bytes=64)
+    scales = keep.tile([P, PASSES * P], U8, name="scales_" + label, align_bytes=64)
+    nc.vector.quantize_mx(out=codes[:].bitcast(FP8X4), scales=scales[:], in_=grouped[:])
+    return codes, scales
+
+
+def project(nc, sums_pool, weights, proposals):
+    sums = sums_pool.tile([P, PACK, P], F32, tag="sums")
+    h_codes, h_scales = proposals
+    for t in range(PACK):
+        w_codes, w_scales = weights[t]
+        for g in range(PASSES):
+            cols = slice(g * P, (g + 1) * P)
+            nc.tensor.matmul_mx(
+                out=sums[:, t, :],
+                lhsT=w_codes[:, cols].bitcast(FP8X4),
+                lhsT_scale=w_scales[:, cols],
+                rhs=h_codes[:, cols].bitcast(FP8X4),
+                rhs_scale=h_scales[:, cols],
+                start=(g == 0),
+                stop=(g == PASSES - 1),
+            )
+    return sums
+
+
+def tile_selsahead_pb_kernel(tc, h, w_q, b_q, w_k, b_k, out):
+    nc = tc.nc
+    weight_dram = {"q": w_q, "k": w_k}
+    bias_dram = {"q": b_q, "k": b_k}
+    quarters = [("k", 0), ("q", 0), ("k", 1), ("q", 1)]
+
+    with ExitStack() as ctx:
+        ctx.enter_context(tc.manual_schedule())
+        keep = ctx.enter_context(tc.tile_pool(name="keep", bufs=1))
+        turned_pool = ctx.enter_context(tc.psum_pool(name="turned", bufs=4))
+        sums_pool = ctx.enter_context(tc.psum_pool(name="sums", bufs=4))
+
+        identity = keep.tile([P, P], F32, name="identity")
+        make_identity(nc, identity[:])
+
+        bias = {}
+        for m in ("k", "q"):
+            bias[m] = keep.tile([P, PASSES, PACK], BF16, name="bias_" + m)
+            nc.scalar.dma_start(
+                out=bias[m][:],
+                in_=bias_dram[m].rearrange("(g p t) -> p g t", g=PASSES, p=P, t=PACK),
+            )
+        h_raw = []
+        for i in range(GROUPS):
+            raw = keep.tile([P, FEATURES], BF16, name="h_raw_%d" % i)
+            nc.sync.dma_start(out=raw[:], in_=h[i * P : (i + 1) * P, :])
+            h_raw.append(raw)
+        w_raw = {}
+        for m, half in quarters:
+            rows = weight_dram[m].rearrange("(g p t) d -> g p t d", g=PASSES, p=P, t=PACK)
+            for j in range(PACK // LOAD_ROWS):
+                raw = keep.tile([P, LOAD_ROWS, FEATURES], BF16, name="w_raw_%s%d_%d" % (m, half, j))
+                nc.sync.dma_start(
+                    out=raw[:], in_=rows[half, :, j * LOAD_ROWS : (j + 1) * LOAD_ROWS, :]
+                )
+                for jj in range(LOAD_ROWS):
+                    w_raw[(m, half, j * LOAD_ROWS + jj)] = raw[:, jj, :]
+
+        qk_codes = {}
+        qk_scales = {}
+        for m, half in quarters:
+            qk_codes[(m, half)] = keep.tile(
+                [P, PROPOSALS], U32, name="codes_%s%d" % (m, half), align_bytes=64
+            )
+            qk_scales[(m, half)] = keep.tile(
+                [P, PROPOSALS], U8, name="scales_%s%d" % (m, half), align_bytes=64
+            )
+
+        def transpose_quarter(m, half):
+            return [
+                transpose_rows(
+                    nc, turned_pool, keep, w_raw[(m, half, t)], identity, "%s%d_%d" % (m, half, t)
+                )
+                for t in range(PACK)
+            ]
+
+        def affinity(i):
+            logits = turned_pool.tile([P, PROPOSALS], F32, tag="bank")
+            cols = slice(i * P, (i + 1) * P)
+            for half in range(PASSES):
+                nc.tensor.matmul_mx(
+                    out=logits[:],
+                    lhsT=qk_codes[("q", half)][:, cols].bitcast(FP8X4),
+                    lhsT_scale=qk_scales[("q", half)][:, cols],
+                    rhs=qk_codes[("k", half)][:].bitcast(FP8X4),
+                    rhs_scale=qk_scales[("k", half)][:],
+                    start=(half == 0),
+                    stop=(half == PASSES - 1),
+                )
+            scaled = keep.tile([P, PROPOSALS], F32, name="scaled_%d" % i)
+            nc.scalar.mul(out=scaled[:], in_=logits[:], mul=SCALE)
+            nc.sync.dma_start(out=out[cols, :], in_=scaled[:])
+
+        h_grouped = [
+            transpose_rows(nc, turned_pool, keep, h_raw[i][:], identity, "h%d" % i)
+            for i in range(GROUPS)
+        ]
+        h_mx = [quantise_rows(nc, keep, h_grouped[i], "h%d" % i) for i in range(GROUPS)]
+        next_grouped = transpose_quarter(*quarters[0])
+        next_mx = [
+            quantise_rows(nc, keep, next_grouped[t], "%s%d_%d" % (quarters[0] + (t,)))
+            for t in range(PACK)
+        ]
+
+        for step, (m, half) in enumerate(quarters):
+            last = step == len(quarters) - 1
+            this_mx = next_mx
+            if not last:
+                next_grouped = transpose_quarter(*quarters[step + 1])
+                next_mx = []
+            for i in range(GROUPS):
+                sums = project(nc, sums_pool, this_mx, h_mx[i])
+                rounded = keep.tile(
+                    [P, P * PACK], BF16, name="rounded_%s%d_%d" % (m, half, i), align_bytes=64
+                )
+                nc.vector.tensor_tensor(
+                    out=rounded[:].rearrange("p (n t) -> p n t", t=PACK),
+                    in0=sums[:].rearrange("p t n -> p n t"),
+                    in1=bias[m][:, half, :].unsqueeze(1).to_broadcast([P, P, PACK]),
+                    op=mybir.AluOpType.add,
+                )
+                if not last:
+                    next_mx.append(
+                        quantise_rows(
+                            nc, keep, next_grouped[i], "%s%d_%d" % (quarters[step + 1] + (i,))
+                        )
+                    )
+                cols = slice(i * P, (i + 1) * P)
+                nc.vector.quantize_mx(
+                    out=qk_codes[(m, half)][:, cols].bitcast(FP8X4),
+                    scales=qk_scales[(m, half)][:, cols],
+                    in_=rounded[:],
+                )
+                if last and i >= 1:
+                    affinity(i - 1)
+        affinity(GROUPS - 1)

@@ -18,32 +18,41 @@ FEATURES = 1024
 PASSES = FEATURES // K_PASS
 GROUPS = PROPOSALS // P
 WORDS = FEATURES // 2
+TILE_WORDS = PASSES * P
 LOAD_ROWS = 2
+LOADS = PACK // LOAD_ROWS
 SCALE = 1.0 / math.sqrt(FEATURES)
-assert GROUPS == PACK
 
 FLOPS = 2 * 2 * PROPOSALS * FEATURES * FEATURES + 2 * PROPOSALS * PROPOSALS * FEATURES
 
 
-def transpose_rows(nc, turned_pool, keep, rows, identity, label):
-    words = rows.bitcast(F32)
-    turned = turned_pool.tile([P, WORDS], F32, tag="bank")
-    for c in range(WORDS // P):
-        cols = slice(c * P, (c + 1) * P)
-        nc.tensor.transpose(turned[:, cols], words[:, cols], identity[:])
-    grouped = keep.tile([P, FEATURES], BF16, name="grouped_" + label, align_bytes=64)
-    nc.scalar.copy(
-        out=grouped[:].bitcast(F32).rearrange("p (g r u) -> p g r u", g=PASSES, u=2),
-        in_=turned[:].rearrange("p (g u r) -> p g r u", g=PASSES, u=2),
-    )
+def transpose_rows(nc, banks, keep, raw, identity, label):
+    count = raw[:].shape[1]
+    grouped = keep.tile([P, count * FEATURES], BF16, name="grouped_" + label, align_bytes=64)
+    for c in range(count):
+        words = raw[:, c, :].bitcast(F32)
+        turned = banks.tile([P, WORDS], F32, tag="bank")
+        for b in range(WORDS // P):
+            cols = slice(b * P, (b + 1) * P)
+            nc.tensor.transpose(turned[:, cols], words[:, cols], identity[:])
+        nc.scalar.copy(
+            out=grouped[:, c * FEATURES : (c + 1) * FEATURES]
+            .bitcast(F32)
+            .rearrange("p (g r u) -> p g r u", g=PASSES, u=2),
+            in_=turned[:].rearrange("p (g u r) -> p g r u", g=PASSES, u=2),
+        )
     return grouped
 
 
 def quantise_rows(nc, keep, grouped, label):
-    codes = keep.tile([P, PASSES * P], U32, name="codes_" + label, align_bytes=64)
-    scales = keep.tile([P, PASSES * P], U8, name="scales_" + label, align_bytes=64)
+    width = grouped[:].shape[1] // PACK
+    codes = keep.tile([P, width], U32, name="codes_" + label, align_bytes=64)
+    scales = keep.tile([P, width], U8, name="scales_" + label, align_bytes=64)
     nc.vector.quantize_mx(out=codes[:].bitcast(FP8X4), scales=scales[:], in_=grouped[:])
-    return codes, scales
+    return [
+        (codes[:, c : c + TILE_WORDS], scales[:, c : c + TILE_WORDS])
+        for c in range(0, width, TILE_WORDS)
+    ]
 
 
 def project(nc, sums_pool, weights, proposals):
@@ -74,7 +83,7 @@ def tile_selsahead_pb_kernel(tc, h, w_q, b_q, w_k, b_k, out):
     with ExitStack() as ctx:
         ctx.enter_context(tc.manual_schedule())
         keep = ctx.enter_context(tc.tile_pool(name="keep", bufs=1))
-        turned_pool = ctx.enter_context(tc.psum_pool(name="turned", bufs=4))
+        banks = ctx.enter_context(tc.psum_pool(name="banks", bufs=4))
         sums_pool = ctx.enter_context(tc.psum_pool(name="sums", bufs=4))
 
         identity = keep.tile([P, P], F32, name="identity")
@@ -87,21 +96,26 @@ def tile_selsahead_pb_kernel(tc, h, w_q, b_q, w_k, b_k, out):
                 out=bias[m][:],
                 in_=bias_dram[m].rearrange("(g p t) -> p g t", g=PASSES, p=P, t=PACK),
             )
-        h_raw = []
-        for i in range(GROUPS):
-            raw = keep.tile([P, FEATURES], BF16, name="h_raw_%d" % i)
-            nc.sync.dma_start(out=raw[:], in_=h[i * P : (i + 1) * P, :])
-            h_raw.append(raw)
-        w_raw = {}
-        for m, half in quarters:
+
+        def load_quarter(m, half):
             rows = weight_dram[m].rearrange("(g p t) d -> g p t d", g=PASSES, p=P, t=PACK)
-            for j in range(PACK // LOAD_ROWS):
-                raw = keep.tile([P, LOAD_ROWS, FEATURES], BF16, name="w_raw_%s%d_%d" % (m, half, j))
+            loaded = []
+            for j in range(LOADS):
+                raw = keep.tile([P, LOAD_ROWS, FEATURES], BF16, name="raw_%s%d_%d" % (m, half, j))
                 nc.sync.dma_start(
                     out=raw[:], in_=rows[half, :, j * LOAD_ROWS : (j + 1) * LOAD_ROWS, :]
                 )
-                for jj in range(LOAD_ROWS):
-                    w_raw[(m, half, j * LOAD_ROWS + jj)] = raw[:, jj, :]
+                loaded.append(raw)
+            return loaded
+
+        w_raw = {quarters[0]: load_quarter(*quarters[0])}
+        h_raw = []
+        for i in range(GROUPS):
+            raw = keep.tile([P, 1, FEATURES], BF16, name="raw_h%d" % i)
+            nc.sync.dma_start(out=raw[:, 0, :], in_=h[i * P : (i + 1) * P, :])
+            h_raw.append(raw)
+        for quarter in quarters[1:]:
+            w_raw[quarter] = load_quarter(*quarter)
 
         qk_codes = {}
         qk_scales = {}
@@ -113,71 +127,75 @@ def tile_selsahead_pb_kernel(tc, h, w_q, b_q, w_k, b_k, out):
                 [P, PROPOSALS], U8, name="scales_%s%d" % (m, half), align_bytes=64
             )
 
-        def transpose_quarter(m, half):
+        def transpose_quarter(quarter):
             return [
-                transpose_rows(
-                    nc, turned_pool, keep, w_raw[(m, half, t)], identity, "%s%d_%d" % (m, half, t)
-                )
-                for t in range(PACK)
+                transpose_rows(nc, banks, keep, w_raw[quarter][j], identity, "%s%d_%d" % (quarter + (j,)))
+                for j in range(LOADS)
             ]
 
-        def affinity(i):
-            logits = turned_pool.tile([P, PROPOSALS], F32, tag="bank")
+        def quantise_load(quarter, grouped, j):
+            return quantise_rows(nc, keep, grouped[j], "%s%d_%d" % (quarter + (j,)))
+
+        def affinity_pass(logits, i, half):
             cols = slice(i * P, (i + 1) * P)
-            for half in range(PASSES):
-                nc.tensor.matmul_mx(
-                    out=logits[:],
-                    lhsT=qk_codes[("q", half)][:, cols].bitcast(FP8X4),
-                    lhsT_scale=qk_scales[("q", half)][:, cols],
-                    rhs=qk_codes[("k", half)][:].bitcast(FP8X4),
-                    rhs_scale=qk_scales[("k", half)][:],
-                    start=(half == 0),
-                    stop=(half == PASSES - 1),
-                )
-            scaled = keep.tile([P, PROPOSALS], F32, name="scaled_%d" % i)
-            nc.scalar.mul(out=scaled[:], in_=logits[:], mul=SCALE)
-            nc.sync.dma_start(out=out[cols, :], in_=scaled[:])
+            nc.tensor.matmul_mx(
+                out=logits[:],
+                lhsT=qk_codes[("q", half)][:, cols].bitcast(FP8X4),
+                lhsT_scale=qk_scales[("q", half)][:, cols],
+                rhs=qk_codes[("k", half)][:].bitcast(FP8X4),
+                rhs_scale=qk_scales[("k", half)][:],
+                start=(half == 0),
+                stop=(half == PASSES - 1),
+            )
 
-        h_grouped = [
-            transpose_rows(nc, turned_pool, keep, h_raw[i][:], identity, "h%d" % i)
-            for i in range(GROUPS)
-        ]
-        h_mx = [quantise_rows(nc, keep, h_grouped[i], "h%d" % i) for i in range(GROUPS)]
-        next_grouped = transpose_quarter(*quarters[0])
-        next_mx = [
-            quantise_rows(nc, keep, next_grouped[t], "%s%d_%d" % (quarters[0] + (t,)))
-            for t in range(PACK)
-        ]
+        grouped = transpose_quarter(quarters[0])
+        next_mx = []
+        for j in range(LOADS):
+            next_mx.extend(quantise_load(quarters[0], grouped, j))
+        h_mx = []
+        for i in range(GROUPS):
+            h_grouped = transpose_rows(nc, banks, keep, h_raw[i], identity, "h%d" % i)
+            h_mx.extend(quantise_rows(nc, keep, h_grouped, "h%d" % i))
 
+        logits = []
         for step, (m, half) in enumerate(quarters):
             last = step == len(quarters) - 1
             this_mx = next_mx
-            if not last:
-                next_grouped = transpose_quarter(*quarters[step + 1])
-                next_mx = []
-            for i in range(GROUPS):
-                sums = project(nc, sums_pool, this_mx, h_mx[i])
-                rounded = keep.tile(
-                    [P, P * PACK], BF16, name="rounded_%s%d_%d" % (m, half, i), align_bytes=64
-                )
-                nc.vector.tensor_tensor(
-                    out=rounded[:].rearrange("p (n t) -> p n t", t=PACK),
-                    in0=sums[:].rearrange("p t n -> p n t"),
-                    in1=bias[m][:, half, :].unsqueeze(1).to_broadcast([P, P, PACK]),
-                    op=mybir.AluOpType.add,
-                )
-                if not last:
-                    next_mx.append(
-                        quantise_rows(
-                            nc, keep, next_grouped[i], "%s%d_%d" % (quarters[step + 1] + (i,))
-                        )
-                    )
+            next_mx = []
+            if last:
+                for i in range(GROUPS):
+                    logits.append(banks.tile([P, PROPOSALS], F32, tag="bank", name="logits_%d" % i))
+                    affinity_pass(logits[i], i, 0)
+            else:
+                grouped = transpose_quarter(quarters[step + 1])
+
+            def finish_group(i):
                 cols = slice(i * P, (i + 1) * P)
                 nc.vector.quantize_mx(
                     out=qk_codes[(m, half)][:, cols].bitcast(FP8X4),
                     scales=qk_scales[(m, half)][:, cols],
-                    in_=rounded[:],
+                    in_=rounded[i][:],
                 )
-                if last and i >= 1:
-                    affinity(i - 1)
-        affinity(GROUPS - 1)
+                if last:
+                    affinity_pass(logits[i], i, 1)
+                    scaled = keep.tile([P, PROPOSALS], F32, name="scaled_%d" % i)
+                    nc.scalar.mul(out=scaled[:], in_=logits[i][:], mul=SCALE)
+                    nc.sync.dma_start(out=out[cols, :], in_=scaled[:])
+
+            rounded = []
+            for i in range(GROUPS):
+                if not last and i % (GROUPS // LOADS) == 0:
+                    next_mx.extend(quantise_load(quarters[step + 1], grouped, i // (GROUPS // LOADS)))
+                sums = project(nc, sums_pool, this_mx, h_mx[i])
+                rounded.append(
+                    keep.tile([P, P * PACK], BF16, name="rounded_%s%d_%d" % (m, half, i), align_bytes=64)
+                )
+                nc.vector.tensor_tensor(
+                    out=rounded[i][:].rearrange("p (n t) -> p n t", t=PACK),
+                    in0=sums[:].rearrange("p t n -> p n t"),
+                    in1=bias[m][:, half, :].unsqueeze(1).to_broadcast([P, P, PACK]),
+                    op=mybir.AluOpType.add,
+                )
+                if i >= 1:
+                    finish_group(i - 1)
+            finish_group(GROUPS - 1)

@@ -182,17 +182,18 @@ def tile_selsahead_pb_kernel(tc, h, w_q, b_q, w_k, b_k, out):
                     nc.scalar.mul(out=scaled[:], in_=logits[i][:], mul=SCALE)
                     nc.sync.dma_start(out=out[cols, :], in_=scaled[:])
 
+            sums = [project(nc, sums_pool, this_mx, h_mx[i]) for i in range(GROUPS)]
+
             rounded = []
             for i in range(GROUPS):
                 if not last and i % (GROUPS // LOADS) == 0:
                     next_mx.extend(quantise_load(quarters[step + 1], grouped, i // (GROUPS // LOADS)))
-                sums = project(nc, sums_pool, this_mx, h_mx[i])
                 rounded.append(
                     keep.tile([P, P * PACK], BF16, name="rounded_%s%d_%d" % (m, half, i), align_bytes=64)
                 )
                 nc.vector.tensor_tensor(
                     out=rounded[i][:].rearrange("p (n t) -> p n t", t=PACK),
-                    in0=sums[:].rearrange("p t n -> p n t"),
+                    in0=sums[i][:].rearrange("p t n -> p n t"),
                     in1=bias[m][:, half, :].unsqueeze(1).to_broadcast([P, P, PACK]),
                     op=mybir.AluOpType.add,
                 )

@@ -17,10 +17,14 @@ PROPOSALS = 512
 FEATURES = 1024
 PASSES = FEATURES // K_PASS
 GROUPS = PROPOSALS // P
-WORDS = FEATURES // 2
+PAIRS = FEATURES // 2
+PAIRS_IN_WORD = PACK // 2
 TILE_WORDS = PASSES * P
 LOAD_ROWS = 2
 LOADS = PACK // LOAD_ROWS
+FIRST_LEAD = 2
+PSUM_BANKS = 8
+MX_ALIGN = 64
 SCALE = 1.0 / math.sqrt(FEATURES)
 
 FLOPS = 2 * 2 * PROPOSALS * FEATURES * FEATURES + 2 * PROPOSALS * PROPOSALS * FEATURES
@@ -28,30 +32,30 @@ FLOPS = 2 * 2 * PROPOSALS * FEATURES * FEATURES + 2 * PROPOSALS * PROPOSALS * FE
 
 def transpose_rows(nc, banks, keep, raw, identity, label):
     count = raw[:].shape[1]
-    grouped = keep.tile([P, count * FEATURES], BF16, name="grouped_" + label, align_bytes=64)
+    grouped = keep.tile([P, count * FEATURES], BF16, name="grouped_" + label, align_bytes=MX_ALIGN)
     for c in range(count):
-        words = raw[:, c, :].bitcast(F32)
-        turned = banks.tile([P, WORDS], F32, tag="bank")
-        for b in range(WORDS // P):
-            cols = slice(b * P, (b + 1) * P)
-            nc.tensor.transpose(turned[:, cols], words[:, cols], identity[:])
+        pairs = raw[:, c, :].bitcast(F32)
+        turned = banks.tile([P, PAIRS], F32, tag="bank")
+        for block in range(PAIRS // P):
+            cols = slice(block * P, (block + 1) * P)
+            nc.tensor.transpose(turned[:, cols], pairs[:, cols], identity[:])
         nc.scalar.copy(
             out=grouped[:, c * FEATURES : (c + 1) * FEATURES]
             .bitcast(F32)
-            .rearrange("p (g r u) -> p g r u", g=PASSES, u=2),
-            in_=turned[:].rearrange("p (g u r) -> p g r u", g=PASSES, u=2),
+            .rearrange("p (g r u) -> p g r u", g=PASSES, u=PAIRS_IN_WORD),
+            in_=turned[:].rearrange("p (g u r) -> p g r u", g=PASSES, u=PAIRS_IN_WORD),
         )
     return grouped
 
 
 def quantise_rows(nc, keep, grouped, label):
     width = grouped[:].shape[1] // PACK
-    codes = keep.tile([P, width], U32, name="codes_" + label, align_bytes=64)
-    scales = keep.tile([P, width], U8, name="scales_" + label, align_bytes=64)
+    codes = keep.tile([P, width], U32, name="codes_" + label, align_bytes=MX_ALIGN)
+    scales = keep.tile([P, width], U8, name="scales_" + label, align_bytes=MX_ALIGN)
     nc.vector.quantize_mx(out=codes[:].bitcast(FP8X4), scales=scales[:], in_=grouped[:])
     return [
-        (codes[:, c : c + TILE_WORDS], scales[:, c : c + TILE_WORDS])
-        for c in range(0, width, TILE_WORDS)
+        (codes[:, first : first + TILE_WORDS], scales[:, first : first + TILE_WORDS])
+        for first in range(0, width, TILE_WORDS)
     ]
 
 
@@ -83,8 +87,8 @@ def tile_selsahead_pb_kernel(tc, h, w_q, b_q, w_k, b_k, out):
     with ExitStack() as ctx:
         ctx.enter_context(tc.manual_schedule())
         keep = ctx.enter_context(tc.tile_pool(name="keep", bufs=1))
-        banks = ctx.enter_context(tc.psum_pool(name="banks", bufs=4))
-        sums_pool = ctx.enter_context(tc.psum_pool(name="sums", bufs=4))
+        banks = ctx.enter_context(tc.psum_pool(name="banks", bufs=PSUM_BANKS // 2))
+        sums_pool = ctx.enter_context(tc.psum_pool(name="sums", bufs=PSUM_BANKS // 2))
 
         identity = keep.tile([P, P], F32, name="identity")
         make_identity(nc, identity[:])
@@ -97,13 +101,13 @@ def tile_selsahead_pb_kernel(tc, h, w_q, b_q, w_k, b_k, out):
                 in_=bias_dram[m].rearrange("(g p t) -> p g t", g=PASSES, p=P, t=PACK),
             )
 
-        def load_quarter(m, half):
+        def load_quarter(m, f_pass):
             rows = weight_dram[m].rearrange("(g p t) d -> g p t d", g=PASSES, p=P, t=PACK)
             loaded = []
             for j in range(LOADS):
-                raw = keep.tile([P, LOAD_ROWS, FEATURES], BF16, name="raw_%s%d_%d" % (m, half, j))
+                raw = keep.tile([P, LOAD_ROWS, FEATURES], BF16, name="raw_%s%d_%d" % (m, f_pass, j))
                 nc.sync.dma_start(
-                    out=raw[:], in_=rows[half, :, j * LOAD_ROWS : (j + 1) * LOAD_ROWS, :]
+                    out=raw[:], in_=rows[f_pass, :, j * LOAD_ROWS : (j + 1) * LOAD_ROWS, :]
                 )
                 loaded.append(raw)
             return loaded
@@ -119,12 +123,12 @@ def tile_selsahead_pb_kernel(tc, h, w_q, b_q, w_k, b_k, out):
 
         qk_codes = {}
         qk_scales = {}
-        for m, half in quarters:
-            qk_codes[(m, half)] = keep.tile(
-                [P, PROPOSALS], U32, name="codes_%s%d" % (m, half), align_bytes=64
+        for m, f_pass in quarters:
+            qk_codes[(m, f_pass)] = keep.tile(
+                [P, PROPOSALS], U32, name="codes_%s%d" % (m, f_pass), align_bytes=MX_ALIGN
             )
-            qk_scales[(m, half)] = keep.tile(
-                [P, PROPOSALS], U8, name="scales_%s%d" % (m, half), align_bytes=64
+            qk_scales[(m, f_pass)] = keep.tile(
+                [P, PROPOSALS], U8, name="scales_%s%d" % (m, f_pass), align_bytes=MX_ALIGN
             )
 
         def transpose_quarter(quarter):
@@ -133,47 +137,50 @@ def tile_selsahead_pb_kernel(tc, h, w_q, b_q, w_k, b_k, out):
                 for j in range(LOADS)
             ]
 
-        def quantise_load(quarter, grouped, j):
-            return quantise_rows(nc, keep, grouped[j], "%s%d_%d" % (quarter + (j,)))
+        def quantise_load(quarter, quarter_grouped, j):
+            return quantise_rows(nc, keep, quarter_grouped[j], "%s%d_%d" % (quarter + (j,)))
 
-        def affinity_pass(logits, i, half):
+        def affinity_pass(logits_i, i, f_pass):
             cols = slice(i * P, (i + 1) * P)
             nc.tensor.matmul_mx(
-                out=logits[:],
-                lhsT=qk_codes[("q", half)][:, cols].bitcast(FP8X4),
-                lhsT_scale=qk_scales[("q", half)][:, cols],
-                rhs=qk_codes[("k", half)][:].bitcast(FP8X4),
-                rhs_scale=qk_scales[("k", half)][:],
-                start=(half == 0),
-                stop=(half == PASSES - 1),
+                out=logits_i[:],
+                lhsT=qk_codes[("q", f_pass)][:, cols].bitcast(FP8X4),
+                lhsT_scale=qk_scales[("q", f_pass)][:, cols],
+                rhs=qk_codes[("k", f_pass)][:].bitcast(FP8X4),
+                rhs_scale=qk_scales[("k", f_pass)][:],
+                start=(f_pass == 0),
+                stop=(f_pass == PASSES - 1),
             )
 
-        grouped = transpose_quarter(quarters[0])
+        next_grouped = transpose_quarter(quarters[0])
         next_mx = []
         for j in range(LOADS):
-            next_mx.extend(quantise_load(quarters[0], grouped, j))
+            next_mx.extend(quantise_load(quarters[0], next_grouped, j))
         h_mx = []
         for i in range(GROUPS):
             h_grouped = transpose_rows(nc, banks, keep, h_raw[i], identity, "h%d" % i)
             h_mx.extend(quantise_rows(nc, keep, h_grouped, "h%d" % i))
 
         logits = []
-        for step, (m, half) in enumerate(quarters):
+        for step, (m, f_pass) in enumerate(quarters):
             last = step == len(quarters) - 1
             this_mx = next_mx
             next_mx = []
+            lead = FIRST_LEAD if step == 0 else 0
+            products = [project(nc, sums_pool, this_mx, h_mx[i]) for i in range(lead)]
             if last:
                 for i in range(GROUPS):
                     logits.append(banks.tile([P, PROPOSALS], F32, tag="bank", name="logits_%d" % i))
                     affinity_pass(logits[i], i, 0)
             else:
-                grouped = transpose_quarter(quarters[step + 1])
+                next_grouped = transpose_quarter(quarters[step + 1])
+            products.extend([project(nc, sums_pool, this_mx, h_mx[i]) for i in range(lead, GROUPS)])
 
             def finish_group(i):
                 cols = slice(i * P, (i + 1) * P)
                 nc.vector.quantize_mx(
-                    out=qk_codes[(m, half)][:, cols].bitcast(FP8X4),
-                    scales=qk_scales[(m, half)][:, cols],
+                    out=qk_codes[(m, f_pass)][:, cols].bitcast(FP8X4),
+                    scales=qk_scales[(m, f_pass)][:, cols],
                     in_=rounded[i][:],
                 )
                 if last:
@@ -182,19 +189,20 @@ def tile_selsahead_pb_kernel(tc, h, w_q, b_q, w_k, b_k, out):
                     nc.scalar.mul(out=scaled[:], in_=logits[i][:], mul=SCALE)
                     nc.sync.dma_start(out=out[cols, :], in_=scaled[:])
 
-            sums = [project(nc, sums_pool, this_mx, h_mx[i]) for i in range(GROUPS)]
-
             rounded = []
             for i in range(GROUPS):
-                if not last and i % (GROUPS // LOADS) == 0:
-                    next_mx.extend(quantise_load(quarters[step + 1], grouped, i // (GROUPS // LOADS)))
+                j = i - lead
+                if not last and 0 <= j < LOADS:
+                    next_mx.extend(quantise_load(quarters[step + 1], next_grouped, j))
                 rounded.append(
-                    keep.tile([P, P * PACK], BF16, name="rounded_%s%d_%d" % (m, half, i), align_bytes=64)
+                    keep.tile(
+                        [P, P * PACK], BF16, name="rounded_%s%d_%d" % (m, f_pass, i), align_bytes=MX_ALIGN
+                    )
                 )
                 nc.vector.tensor_tensor(
                     out=rounded[i][:].rearrange("p (n t) -> p n t", t=PACK),
-                    in0=sums[i][:].rearrange("p t n -> p n t"),
-                    in1=bias[m][:, half, :].unsqueeze(1).to_broadcast([P, P, PACK]),
+                    in0=products[i][:].rearrange("p t n -> p n t"),
+                    in1=bias[m][:, f_pass, :].unsqueeze(1).to_broadcast([P, P, PACK]),
                     op=mybir.AluOpType.add,
                 )
                 if i >= 1:

from contextlib import ExitStack
import math

import concourse.mybir as mybir
from concourse.masks import make_identity

F32 = mybir.dt.float32
BF16 = mybir.dt.bfloat16
U32 = mybir.dt.uint32
U8 = mybir.dt.uint8
FP8X4 = mybir.dt.float8_e4m3fn_x4

P = 128
PACK = 4
K_PASS = P * PACK
PROPOSALS = 512
FEATURES = 1024
PASSES = FEATURES // K_PASS
GROUPS = PROPOSALS // P
PAIRS = FEATURES // 2
PAIRS_IN_WORD = PACK // 2
TILE_WORDS = PASSES * P
LOAD_ROWS = 2
LOADS = PACK // LOAD_ROWS
FIRST_LEAD = 2
PSUM_BANKS = 8
MX_ALIGN = 64
SCALE = 1.0 / math.sqrt(FEATURES)

FLOPS = 2 * 2 * PROPOSALS * FEATURES * FEATURES + 2 * PROPOSALS * PROPOSALS * FEATURES


def transpose_rows(nc, banks, keep, raw, identity, label):
    count = raw[:].shape[1]
    grouped = keep.tile([P, count * FEATURES], BF16, name="grouped_" + label, align_bytes=MX_ALIGN)
    for c in range(count):
        pairs = raw[:, c, :].bitcast(F32)
        turned = banks.tile([P, PAIRS], F32, tag="bank")
        for block in range(PAIRS // P):
            cols = slice(block * P, (block + 1) * P)
            nc.tensor.transpose(turned[:, cols], pairs[:, cols], identity[:])
        nc.scalar.copy(
            out=grouped[:, c * FEATURES : (c + 1) * FEATURES]
            .bitcast(F32)
            .rearrange("p (g r u) -> p g r u", g=PASSES, u=PAIRS_IN_WORD),
            in_=turned[:].rearrange("p (g u r) -> p g r u", g=PASSES, u=PAIRS_IN_WORD),
        )
    return grouped


def quantise_rows(nc, keep, grouped, label):
    width = grouped[:].shape[1] // PACK
    codes = keep.tile([P, width], U32, name="codes_" + label, align_bytes=MX_ALIGN)
    scales = keep.tile([P, width], U8, name="scales_" + label, align_bytes=MX_ALIGN)
    nc.vector.quantize_mx(out=codes[:].bitcast(FP8X4), scales=scales[:], in_=grouped[:])
    return [
        (codes[:, first : first + TILE_WORDS], scales[:, first : first + TILE_WORDS])
        for first in range(0, width, TILE_WORDS)
    ]


def project(nc, sums_pool, weights, proposals):
    sums = sums_pool.tile([P, PACK, P], F32, tag="sums")
    h_codes, h_scales = proposals
    for t in range(PACK):
        w_codes, w_scales = weights[t]
        for g in range(PASSES):
            cols = slice(g * P, (g + 1) * P)
            nc.tensor.matmul_mx(
                out=sums[:, t, :],
                lhsT=w_codes[:, cols].bitcast(FP8X4),
                lhsT_scale=w_scales[:, cols],
                rhs=h_codes[:, cols].bitcast(FP8X4),
                rhs_scale=h_scales[:, cols],
                start=(g == 0),
                stop=(g == PASSES - 1),
            )
    return sums


def tile_selsahead_pb_kernel(tc, h, w_q, b_q, w_k, b_k, out):
    nc = tc.nc
    weight_dram = {"q": w_q, "k": w_k}
    bias_dram = {"q": b_q, "k": b_k}
    quarters = [("k", 0), ("q", 0), ("k", 1), ("q", 1)]

    with ExitStack() as ctx:
        ctx.enter_context(tc.manual_schedule())
        keep = ctx.enter_context(tc.tile_pool(name="keep", bufs=1))
        banks = ctx.enter_context(tc.psum_pool(name="banks", bufs=PSUM_BANKS // 2))
        sums_pool = ctx.enter_context(tc.psum_pool(name="sums", bufs=PSUM_BANKS // 2))

        identity = keep.tile([P, P], F32, name="identity")
        make_identity(nc, identity[:])

        bias = {}
        for m in ("k", "q"):
            bias[m] = keep.tile([P, PASSES, PACK], BF16, name="bias_" + m)
            nc.scalar.dma_start(
                out=bias[m][:],
                in_=bias_dram[m].rearrange("(g p t) -> p g t", g=PASSES, p=P, t=PACK),
            )

        def load_quarter(m, f_pass):
            rows = weight_dram[m].rearrange("(g p t) d -> g p t d", g=PASSES, p=P, t=PACK)
            loaded = []
            for j in range(LOADS):
                raw = keep.tile([P, LOAD_ROWS, FEATURES], BF16, name="raw_%s%d_%d" % (m, f_pass, j))
                nc.sync.dma_start(
                    out=raw[:], in_=rows[f_pass, :, j * LOAD_ROWS : (j + 1) * LOAD_ROWS, :]
                )
                loaded.append(raw)
            return loaded

        w_raw = {quarters[0]: load_quarter(*quarters[0])}
        h_raw = []
        for i in range(GROUPS):
            raw = keep.tile([P, 1, FEATURES], BF16, name="raw_h%d" % i)
            nc.sync.dma_start(out=raw[:, 0, :], in_=h[i * P : (i + 1) * P, :])
            h_raw.append(raw)
        for quarter in quarters[1:]:
            w_raw[quarter] = load_quarter(*quarter)

        qk_codes = {}
        qk_scales = {}
        for m, f_pass in quarters:
            qk_codes[(m, f_pass)] = keep.tile(
                [P, PROPOSALS], U32, name="codes_%s%d" % (m, f_pass), align_bytes=MX_ALIGN
            )
            qk_scales[(m, f_pass)] = keep.tile(
                [P, PROPOSALS], U8, name="scales_%s%d" % (m, f_pass), align_bytes=MX_ALIGN
            )

        def transpose_quarter(quarter):
            return [
                transpose_rows(nc, banks, keep, w_raw[quarter][j], identity, "%s%d_%d" % (quarter + (j,)))
                for j in range(LOADS)
            ]

        def quantise_load(quarter, quarter_grouped, j):
            return quantise_rows(nc, keep, quarter_grouped[j], "%s%d_%d" % (quarter + (j,)))

        def affinity_pass(logits_i, i, f_pass):
            cols = slice(i * P, (i + 1) * P)
            nc.tensor.matmul_mx(
                out=logits_i[:],
                lhsT=qk_codes[("q", f_pass)][:, cols].bitcast(FP8X4),
                lhsT_scale=qk_scales[("q", f_pass)][:, cols],
                rhs=qk_codes[("k", f_pass)][:].bitcast(FP8X4),
                rhs_scale=qk_scales[("k", f_pass)][:],
                start=(f_pass == 0),
                stop=(f_pass == PASSES - 1),
            )

        next_grouped = transpose_quarter(quarters[0])
        next_mx = []
        for j in range(LOADS):
            next_mx.extend(quantise_load(quarters[0], next_grouped, j))
        h_mx = []
        for i in range(GROUPS):
            h_grouped = transpose_rows(nc, banks, keep, h_raw[i], identity, "h%d" % i)
            h_mx.extend(quantise_rows(nc, keep, h_grouped, "h%d" % i))

        logits = []
        for step, (m, f_pass) in enumerate(quarters):
            last = step == len(quarters) - 1
            this_mx = next_mx
            next_mx = []
            lead = FIRST_LEAD if step == 0 else 0
            products = [project(nc, sums_pool, this_mx, h_mx[i]) for i in range(lead)]
            if last:
                for i in range(GROUPS):
                    logits.append(banks.tile([P, PROPOSALS], F32, tag="bank", name="logits_%d" % i))
                    affinity_pass(logits[i], i, 0)
            else:
                next_grouped = transpose_quarter(quarters[step + 1])
            products.extend([project(nc, sums_pool, this_mx, h_mx[i]) for i in range(lead, GROUPS)])

            def finish_group(i):
                cols = slice(i * P, (i + 1) * P)
                nc.vector.quantize_mx(
                    out=qk_codes[(m, f_pass)][:, cols].bitcast(FP8X4),
                    scales=qk_scales[(m, f_pass)][:, cols],
                    in_=rounded[i][:],
                )
                if last:
                    affinity_pass(logits[i], i, 1)
                    scaled = keep.tile([P, PROPOSALS], F32, name="scaled_%d" % i)
                    nc.scalar.mul(out=scaled[:], in_=logits[i][:], mul=SCALE)
                    nc.sync.dma_start(out=out[cols, :], in_=scaled[:])

            rounded = []
            for i in range(GROUPS):
                j = i - lead
                if not last and 0 <= j < LOADS:
                    next_mx.extend(quantise_load(quarters[step + 1], next_grouped, j))
                rounded.append(
                    keep.tile(
                        [P, P * PACK], BF16, name="rounded_%s%d_%d" % (m, f_pass, i), align_bytes=MX_ALIGN
                    )
                )
                nc.vector.tensor_tensor(
                    out=rounded[i][:].rearrange("p (n t) -> p n t", t=PACK),
                    in0=products[i][:].rearrange("p t n -> p n t"),
                    in1=bias[m][:, f_pass, :].unsqueeze(1).to_broadcast([P, P, PACK]),
                    op=mybir.AluOpType.add,
                )
                if i >= 1:
                    finish_group(i - 1)
            finish_group(GROUPS - 1)
